import numpy as np
import ml_dtypes


def mxq(x, axis, fmt="e4m3"):
    dtype, down = {"e4m3": (ml_dtypes.float8_e4m3fn, 7), "e5m2": (ml_dtypes.float8_e5m2, 14)}[fmt]
    v = np.moveaxis(np.asarray(x, np.float32).astype(ml_dtypes.bfloat16).astype(np.float64), axis, -1)
    blocks = v.reshape(v.shape[:-1] + (-1, 32))
    amax = np.abs(blocks).max(-1, keepdims=True)
    byte = np.maximum(np.where(amax > 0, np.frexp(amax)[1] - 1 + 127, 0) - down, 1)
    scale = np.exp2(byte - 127.0)
    codes = (blocks / scale).astype(np.float32).astype(dtype).astype(np.float64)
    return np.moveaxis((codes * scale).reshape(v.shape), -1, axis)


WIDE = False


def mx_kscale(k):
    if not WIDE:
        return np.ones(k)
    levels = np.array([10, -10, 5, -5, 0])
    a = np.random.permutation(np.resize(levels, k // 512 * 4)).reshape(k // 512, 4)
    idx = np.arange(k)
    return np.exp2(a[idx // 512, idx % 128 // 32])


BF16 = ml_dtypes.bfloat16


def bf(x):
    return np.asarray(x, np.float32).astype(BF16)


def f64(x):
    return np.asarray(x).astype(np.float64)


E2M1 = np.array([0.0, 0.5, 1.0, 1.5, 2.0, 3.0, 4.0, 6.0, -0.0, -0.5, -1.0, -1.5, -2.0, -3.0, -4.0, -6.0])


def pack_weight(w, fmt):
    k, n = w.shape
    w = f64(bf(w)).reshape(k // 32, 32, n)
    amax = np.abs(w).max(1)
    if fmt == "e4m3":
        byte = np.frexp(amax)[1] - 1 + 127 - 7
    else:
        mant, ex = np.frexp(amax / 6.0)
        byte = np.where(mant > 0.5, ex, ex - 1) + 127
    byte = np.clip(np.where(amax > 0, byte, 1), 1, 254)
    scaled = (w * np.exp2(127.0 - byte)[:, None, :]).reshape(k, n).astype(np.float32)
    by_word = np.ascontiguousarray(scaled.reshape(k // 512, 128, 4, n).transpose(0, 1, 3, 2))
    if fmt == "e4m3":
        words = by_word.astype(ml_dtypes.float8_e4m3fn).view(np.uint8)
    else:
        c = by_word.astype(ml_dtypes.float4_e2m1fn).view(np.uint8) & 0xF
        words = c[..., 0::2] | (c[..., 1::2] << 4)
    return np.ascontiguousarray(words), np.ascontiguousarray(byte.astype(np.uint8).reshape(k // 512, 16, n))


def unpack_weight(words, scales, fmt):
    g, p, n, _ = words.shape
    if fmt == "e4m3":
        vals = np.ascontiguousarray(words).view(ml_dtypes.float8_e4m3fn).astype(np.float64)
    else:
        nib = np.empty((g, p, n, 4), np.uint8)
        nib[..., 0::2] = words & 0xF
        nib[..., 1::2] = words >> 4
        vals = E2M1[nib]
    vals = vals * np.repeat(np.exp2(scales.astype(np.float64) - 127.0), 8, axis=1)[..., None]
    return vals.transpose(0, 1, 3, 2).reshape(g * 512, n)


B, S, H, R = 1, 128, 8192, 4096
G = H // R


def setup_inputs():
    s = mx_kscale(R)
    x = bf(np.random.standard_normal((B, S, H)) * np.tile(s, G))
    words, scales = pack_weight(np.random.standard_normal((R, R)) / np.sqrt(R) / s[:, None], "e4m3")
    return {"x": x, "matrix_words": words, "matrix_scales": scales}


def reference(x, matrix_words, matrix_scales):
    x = f64(x)
    matrix = unpack_weight(matrix_words, matrix_scales, "e4m3")
    b, n, h = x.shape
    r = matrix.shape[0]
    g = h // r
    compressed = x.reshape(b, n, g, r).sum(axis=2)
    out = mxq(compressed, 2, "e4m3") @ matrix
    return np.repeat(out, g, axis=2)[:, :, :h]

@@ -1,0 +1,136 @@
+from contextlib import ExitStack
+
+import concourse.mybir as mybir
+from concourse.masks import make_identity
+
+BF16 = mybir.dt.bfloat16
+F32 = mybir.dt.float32
+I32 = mybir.dt.int32
+U8 = mybir.dt.uint8
+U32 = mybir.dt.uint32
+FP8X4 = mybir.dt.float8_e4m3fn_x4
+
+P = 128
+PACK = 4
+K_PASS = P * PACK
+R = 4096
+GROUPS = 2
+REPEAT = 2
+PASSES = R // K_PASS
+N_BANK = 512
+PSUM_BANKS = 8
+HALVES = 2
+N_HALF = R // HALVES
+BANKS_PER_HALF = N_HALF // N_BANK
+X_PIECES = 2
+K_PIECE = R // X_PIECES
+PASSES_PER_PIECE = K_PIECE // K_PASS
+PLANES_PER_TILE = 4
+PLANE_SETS = PASSES // PLANES_PER_TILE
+QUADRANTS = 4
+SCALE_ROWS = 4
+
+FLOPS = 2 * P * R * R
+
+
+def tile_mora_w_kernel(tc, x, matrix_words, matrix_scales, out):
+    nc = tc.nc
+    x_groups = x.rearrange("b s (h k) -> (b s) h k", h=GROUPS)
+    out_rows = out.rearrange("b s n -> (b s) n")
+
+    with ExitStack() as ctx:
+        keep = ctx.enter_context(tc.tile_pool(name="keep", bufs=1))
+        results = ctx.enter_context(tc.tile_pool(name="results", bufs=HALVES * BANKS_PER_HALF))
+        psum = ctx.enter_context(tc.psum_pool(name="psum", bufs=PSUM_BANKS))
+
+        w_planes = keep.tile([P, PLANE_SETS, R], U8, align_bytes=64)
+        nc.vector.memset(w_planes[:].rearrange("p a n -> p (a n)").bitcast(I32), 0)
+        identity = keep.tile([P, P], BF16)
+        make_identity(nc, identity[:])
+
+        x_tiles = []
+        for j in range(X_PIECES):
+            x_piece = keep.tile([P, GROUPS, K_PIECE], BF16, name="x_piece%d" % j)
+            nc.sync.dma_start(out=x_piece[:], in_=x_groups[:, :, j * K_PIECE : (j + 1) * K_PIECE])
+            x_tiles.append(x_piece)
+
+        for a in range(PLANE_SETS):
+            for quadrant in range(QUADRANTS):
+                first = 32 * quadrant
+                nc.sync.dma_start(
+                    out=w_planes[first : first + PLANES_PER_TILE * SCALE_ROWS, a, :].bitcast(I32),
+                    in_=matrix_scales[
+                        a * PLANES_PER_TILE : (a + 1) * PLANES_PER_TILE,
+                        quadrant * SCALE_ROWS : (quadrant + 1) * SCALE_ROWS,
+                        :,
+                    ].bitcast(I32),
+                )
+
+        w_tiles = []
+        for half in range(HALVES):
+            w_tiles.append([])
+            for g in range(PASSES):
+                w_words = keep.tile([P, N_HALF * PACK], U8, name="w_words%d_%d" % (half, g), align_bytes=64)
+                w_bytes = matrix_words[g].rearrange("p n t -> p (n t)")
+                nc.sync.dma_start(
+                    out=w_words[:].bitcast(I32),
+                    in_=w_bytes[:, half * N_HALF * PACK : (half + 1) * N_HALF * PACK].bitcast(I32),
+                )
+                w_tiles[half].append(w_words)
+
+        c_codes = keep.tile([P, PASSES, P], U32, align_bytes=64)
+        c_scales = keep.tile([P, PASSES, P], U8, align_bytes=64)
+        for j in range(X_PIECES):
+            c = keep.tile([P, K_PIECE], BF16, name="c%d" % j)
+            nc.vector.tensor_tensor(
+                out=c[:], in0=x_tiles[j][:, 0, :], in1=x_tiles[j][:, 1, :], op=mybir.AluOpType.add
+            )
+            grouped = keep.tile([P, PASSES_PER_PIECE, P, PACK], BF16, name="grouped%d" % j, align_bytes=64)
+            for i in range(PASSES_PER_PIECE):
+                c_t = psum.tile([P, PACK, P], BF16, tag="bank")
+                for t in range(PACK):
+                    nc.tensor.transpose(
+                        c_t[:, t, :], c[:, i * K_PASS + t : (i + 1) * K_PASS : PACK], identity[:]
+                    )
+                if i % 2 == 0:
+                    nc.scalar.copy(out=grouped[:, i], in_=c_t[:].rearrange("p t s -> p s t"))
+                else:
+                    nc.vector.tensor_copy(out=grouped[:, i], in_=c_t[:].rearrange("p t s -> p s t"))
+            passes = slice(j * PASSES_PER_PIECE, (j + 1) * PASSES_PER_PIECE)
+            nc.vector.quantize_mx(
+                out=c_codes[:, passes, :].rearrange("p g s -> p (g s)").bitcast(FP8X4),
+                scales=c_scales[:, passes, :].rearrange("p g s -> p (g s)"),
+                in_=grouped[:].rearrange("p g s t -> p (g s t)"),
+            )
+
+        for half in range(HALVES):
+            banks = []
+            for b in range(BANKS_PER_HALF):
+                acc = psum.tile([P, N_BANK], F32, tag="bank", name="acc%d_%d" % (half, b))
+                banks.append(acc)
+            for g in range(PASSES):
+                plane_set = g // PLANES_PER_TILE
+                plane_start = SCALE_ROWS * (g % PLANES_PER_TILE)
+                for b in range(BANKS_PER_HALF):
+                    first_n = half * N_HALF + b * N_BANK
+                    nc.tensor.matmul_mx(
+                        out=banks[b][:],
+                        lhsT=c_codes[:, g, :].bitcast(FP8X4),
+                        lhsT_scale=c_scales[:, g, :],
+                        rhs=w_tiles[half][g][:, b * N_BANK * PACK : (b + 1) * N_BANK * PACK].bitcast(FP8X4),
+                        rhs_scale=w_planes[plane_start:P, plane_set, first_n : first_n + N_BANK],
+                        start=(g == 0),
+                        stop=(g == PASSES - 1),
+                    )
+            for b in range(BANKS_PER_HALF):
+                repeated = results.tile([P, N_BANK, REPEAT], F32)
+                twice = banks[b][:].unsqueeze(2).to_broadcast([P, N_BANK, REPEAT])
+                if b % 2 == 0:
+                    nc.vector.tensor_copy(out=repeated[:], in_=twice)
+                else:
+                    nc.scalar.copy(out=repeated[:], in_=twice)
+                first_out = (half * N_HALF + b * N_BANK) * REPEAT
+                nc.sync.dma_start(
+                    out=out_rows[:, first_out : first_out + N_BANK * REPEAT],
+                    in_=repeated[:].rearrange("p n j -> p (n j)"),
+                )

@@ -57,13 +57,13 @@ def tile_mora_w_kernel(tc, x, matrix_words, matrix_scales, out):
         for a in range(PLANE_SETS):
             for quadrant in range(QUADRANTS):
                 first = 32 * quadrant
-                nc.sync.dma_start(
-                    out=w_planes[first : first + PLANES_PER_TILE * SCALE_ROWS, a, :].bitcast(I32),
+                nc.gpsimd.dma_start(
+                    out=w_planes[first : first + PLANES_PER_TILE * SCALE_ROWS, a, :].bitcast(F32),
                     in_=matrix_scales[
                         a * PLANES_PER_TILE : (a + 1) * PLANES_PER_TILE,
                         quadrant * SCALE_ROWS : (quadrant + 1) * SCALE_ROWS,
                         :,
-                    ].bitcast(I32),
+                    ].bitcast(F32),
                 )
 
         w_tiles = []

@@ -19,9 +19,9 @@ REPEAT = 2
 PASSES = R // K_PASS
 N_BANK = 512
 PSUM_BANKS = 8
-HALVES = 2
-N_HALF = R // HALVES
-BANKS_PER_HALF = N_HALF // N_BANK
+LAST_BANKS = 2
+PART_BANKS = (PSUM_BANKS - LAST_BANKS, LAST_BANKS)
+STORE_BANKS = 2
 X_PIECES = 2
 K_PIECE = R // X_PIECES
 PASSES_PER_PIECE = K_PIECE // K_PASS
@@ -40,7 +40,7 @@ def tile_mora_w_kernel(tc, x, matrix_words, matrix_scales, out):
 
     with ExitStack() as ctx:
         keep = ctx.enter_context(tc.tile_pool(name="keep", bufs=1))
-        results = ctx.enter_context(tc.tile_pool(name="results", bufs=HALVES * BANKS_PER_HALF))
+        results = ctx.enter_context(tc.tile_pool(name="results", bufs=PSUM_BANKS // STORE_BANKS))
         psum = ctx.enter_context(tc.psum_pool(name="psum", bufs=PSUM_BANKS))
 
         w_planes = keep.tile([P, PLANE_SETS, R], U8, align_bytes=64)
@@ -57,26 +57,28 @@ def tile_mora_w_kernel(tc, x, matrix_words, matrix_scales, out):
         for a in range(PLANE_SETS):
             for quadrant in range(QUADRANTS):
                 first = 32 * quadrant
-                nc.gpsimd.dma_start(
-                    out=w_planes[first : first + PLANES_PER_TILE * SCALE_ROWS, a, :].bitcast(F32),
+                nc.sync.dma_start(
+                    out=w_planes[first : first + PLANES_PER_TILE * SCALE_ROWS, a, :].bitcast(I32),
                     in_=matrix_scales[
                         a * PLANES_PER_TILE : (a + 1) * PLANES_PER_TILE,
                         quadrant * SCALE_ROWS : (quadrant + 1) * SCALE_ROWS,
                         :,
-                    ].bitcast(F32),
+                    ].bitcast(I32),
                 )
 
         w_tiles = []
-        for half in range(HALVES):
+        for part in range(len(PART_BANKS)):
+            first_n = sum(PART_BANKS[:part]) * N_BANK
+            part_n = PART_BANKS[part] * N_BANK
             w_tiles.append([])
             for g in range(PASSES):
-                w_words = keep.tile([P, N_HALF * PACK], U8, name="w_words%d_%d" % (half, g), align_bytes=64)
+                w_words = keep.tile([P, part_n * PACK], U8, name="w_words%d_%d" % (part, g), align_bytes=64)
                 w_bytes = matrix_words[g].rearrange("p n t -> p (n t)")
                 nc.sync.dma_start(
                     out=w_words[:].bitcast(I32),
-                    in_=w_bytes[:, half * N_HALF * PACK : (half + 1) * N_HALF * PACK].bitcast(I32),
+                    in_=w_bytes[:, first_n * PACK : (first_n + part_n) * PACK].bitcast(I32),
                 )
-                w_tiles[half].append(w_words)
+                w_tiles[part].append(w_words)
 
         c_codes = keep.tile([P, PASSES, P], U32, align_bytes=64)
         c_scales = keep.tile([P, PASSES, P], U8, align_bytes=64)
@@ -103,34 +105,36 @@ def tile_mora_w_kernel(tc, x, matrix_words, matrix_scales, out):
                 in_=grouped[:].rearrange("p g s t -> p (g s t)"),
             )
 
-        for half in range(HALVES):
+        for part in range(len(PART_BANKS)):
+            first_n = sum(PART_BANKS[:part]) * N_BANK
             banks = []
-            for b in range(BANKS_PER_HALF):
-                acc = psum.tile([P, N_BANK], F32, tag="bank", name="acc%d_%d" % (half, b))
+            for b in range(PART_BANKS[part]):
+                acc = psum.tile([P, N_BANK], F32, tag="bank", name="acc%d_%d" % (part, b))
                 banks.append(acc)
             for g in range(PASSES):
                 plane_set = g // PLANES_PER_TILE
                 plane_start = SCALE_ROWS * (g % PLANES_PER_TILE)
-                for b in range(BANKS_PER_HALF):
-                    first_n = half * N_HALF + b * N_BANK
+                for b in range(PART_BANKS[part]):
+                    bank_n = first_n + b * N_BANK
                     nc.tensor.matmul_mx(
                         out=banks[b][:],
                         lhsT=c_codes[:, g, :].bitcast(FP8X4),
                         lhsT_scale=c_scales[:, g, :],
-                        rhs=w_tiles[half][g][:, b * N_BANK * PACK : (b + 1) * N_BANK * PACK].bitcast(FP8X4),
-                        rhs_scale=w_planes[plane_start:P, plane_set, first_n : first_n + N_BANK],
+                        rhs=w_tiles[part][g][:, b * N_BANK * PACK : (b + 1) * N_BANK * PACK].bitcast(FP8X4),
+                        rhs_scale=w_planes[plane_start:P, plane_set, bank_n : bank_n + N_BANK],
                         start=(g == 0),
                         stop=(g == PASSES - 1),
                     )
-            for b in range(BANKS_PER_HALF):
-                repeated = results.tile([P, N_BANK, REPEAT], F32)
-                twice = banks[b][:].unsqueeze(2).to_broadcast([P, N_BANK, REPEAT])
-                if b % 2 == 0:
-                    nc.vector.tensor_copy(out=repeated[:], in_=twice)
-                else:
-                    nc.scalar.copy(out=repeated[:], in_=twice)
-                first_out = (half * N_HALF + b * N_BANK) * REPEAT
+            for b in range(0, PART_BANKS[part], STORE_BANKS):
+                repeated = results.tile([P, STORE_BANKS, N_BANK, REPEAT], F32)
+                nc.vector.tensor_copy(
+                    out=repeated[:, 0], in_=banks[b][:].unsqueeze(2).to_broadcast([P, N_BANK, REPEAT])
+                )
+                nc.scalar.copy(
+                    out=repeated[:, 1], in_=banks[b + 1][:].unsqueeze(2).to_broadcast([P, N_BANK, REPEAT])
+                )
+                first_out = (first_n + b * N_BANK) * REPEAT
                 nc.sync.dma_start(
-                    out=out_rows[:, first_out : first_out + N_BANK * REPEAT],
-                    in_=repeated[:].rearrange("p n j -> p (n j)"),
+                    out=out_rows[:, first_out : first_out + STORE_BANKS * N_BANK * REPEAT],
+                    in_=repeated[:].rearrange("p b n j -> p (b n j)"),
                 )

@@ -19,8 +19,10 @@ REPEAT = 2
 PASSES = R // K_PASS
 N_BANK = 512
 PSUM_BANKS = 8
-LAST_BANKS = 2
-PART_BANKS = (PSUM_BANKS - LAST_BANKS, LAST_BANKS)
+SPLIT_PASSES = 2
+WHOLE_PASSES = PASSES - SPLIT_PASSES
+PARTS = 2
+PART_BANKS = PSUM_BANKS // PARTS
 STORE_BANKS = 2
 X_PIECES = 2
 K_PIECE = R // X_PIECES
@@ -48,11 +50,8 @@ def tile_mora_w_kernel(tc, x, matrix_words, matrix_scales, out):
         identity = keep.tile([P, P], BF16)
         make_identity(nc, identity[:])
 
-        x_tiles = []
-        for j in range(X_PIECES):
-            x_piece = keep.tile([P, GROUPS, K_PIECE], BF16, name="x_piece%d" % j)
-            nc.sync.dma_start(out=x_piece[:], in_=x_groups[:, :, j * K_PIECE : (j + 1) * K_PIECE])
-            x_tiles.append(x_piece)
+        x_all = keep.tile([P, GROUPS, R], BF16)
+        nc.sync.dma_start(out=x_all[:], in_=x_groups)
 
         for a in range(PLANE_SETS):
             for quadrant in range(QUADRANTS):
@@ -66,26 +65,32 @@ def tile_mora_w_kernel(tc, x, matrix_words, matrix_scales, out):
                     ].bitcast(I32),
                 )
 
-        w_tiles = []
-        for part in range(len(PART_BANKS)):
-            first_n = sum(PART_BANKS[:part]) * N_BANK
-            part_n = PART_BANKS[part] * N_BANK
-            w_tiles.append([])
-            for g in range(PASSES):
-                w_words = keep.tile([P, part_n * PACK], U8, name="w_words%d_%d" % (part, g), align_bytes=64)
-                w_bytes = matrix_words[g].rearrange("p n t -> p (n t)")
-                nc.sync.dma_start(
-                    out=w_words[:].bitcast(I32),
-                    in_=w_bytes[:, first_n * PACK : (first_n + part_n) * PACK].bitcast(I32),
-                )
-                w_tiles[part].append(w_words)
+        def load_words(g, first_bank, banks):
+            w_words = keep.tile(
+                [P, banks * N_BANK * PACK], U8, name="w_words%d_%d" % (g, first_bank), align_bytes=64
+            )
+            w_bytes = matrix_words[g].rearrange("p n t -> p (n t)")
+            first_byte = first_bank * N_BANK * PACK
+            nc.sync.dma_start(
+                out=w_words[:].bitcast(I32),
+                in_=w_bytes[:, first_byte : first_byte + banks * N_BANK * PACK].bitcast(I32),
+            )
+            return w_words
+
+        w_whole = [load_words(g, 0, PSUM_BANKS) for g in range(WHOLE_PASSES)]
+        w_parts = [
+            [load_words(g, part * PART_BANKS, PART_BANKS) for g in range(WHOLE_PASSES, PASSES)]
+            for part in range(PARTS)
+        ]
 
         c_codes = keep.tile([P, PASSES, P], U32, align_bytes=64)
         c_scales = keep.tile([P, PASSES, P], U8, align_bytes=64)
         for j in range(X_PIECES):
             c = keep.tile([P, K_PIECE], BF16, name="c%d" % j)
             nc.vector.tensor_tensor(
-                out=c[:], in0=x_tiles[j][:, 0, :], in1=x_tiles[j][:, 1, :], op=mybir.AluOpType.add
+                out=c[:], in0=x_all[:, 0, j * K_PIECE : (j + 1) * K_PIECE],
+                in1=x_all[:, 1, j * K_PIECE : (j + 1) * K_PIECE],
+                op=mybir.AluOpType.add,
             )
             grouped = keep.tile([P, PASSES_PER_PIECE, P, PACK], BF16, name="grouped%d" % j, align_bytes=64)
             for i in range(PASSES_PER_PIECE):
@@ -105,27 +110,35 @@ def tile_mora_w_kernel(tc, x, matrix_words, matrix_scales, out):
                 in_=grouped[:].rearrange("p g s t -> p (g s t)"),
             )
 
-        for part in range(len(PART_BANKS)):
-            first_n = sum(PART_BANKS[:part]) * N_BANK
-            banks = []
-            for b in range(PART_BANKS[part]):
-                acc = psum.tile([P, N_BANK], F32, tag="bank", name="acc%d_%d" % (part, b))
-                banks.append(acc)
-            for g in range(PASSES):
-                plane_set = g // PLANES_PER_TILE
-                plane_start = SCALE_ROWS * (g % PLANES_PER_TILE)
-                for b in range(PART_BANKS[part]):
-                    bank_n = first_n + b * N_BANK
-                    nc.tensor.matmul_mx(
-                        out=banks[b][:],
-                        lhsT=c_codes[:, g, :].bitcast(FP8X4),
-                        lhsT_scale=c_scales[:, g, :],
-                        rhs=w_tiles[part][g][:, b * N_BANK * PACK : (b + 1) * N_BANK * PACK].bitcast(FP8X4),
-                        rhs_scale=w_planes[plane_start:P, plane_set, bank_n : bank_n + N_BANK],
-                        start=(g == 0),
-                        stop=(g == PASSES - 1),
-                    )
-            for b in range(0, PART_BANKS[part], STORE_BANKS):
+        banks = []
+        for b in range(PSUM_BANKS):
+            acc = psum.tile([P, N_BANK], F32, tag="bank", name="acc%d" % b)
+            banks.append(acc)
+
+        def multiply(g, b, w_words, first_bank):
+            plane_set = g // PLANES_PER_TILE
+            plane_start = SCALE_ROWS * (g % PLANES_PER_TILE)
+            first_byte = (b - first_bank) * N_BANK * PACK
+            nc.tensor.matmul_mx(
+                out=banks[b][:],
+                lhsT=c_codes[:, g, :].bitcast(FP8X4),
+                lhsT_scale=c_scales[:, g, :],
+                rhs=w_words[:, first_byte : first_byte + N_BANK * PACK].bitcast(FP8X4),
+                rhs_scale=w_planes[plane_start:P, plane_set, b * N_BANK : (b + 1) * N_BANK],
+                start=(g == 0),
+                stop=(g == PASSES - 1),
+            )
+
+        for g in range(WHOLE_PASSES):
+            for b in range(PSUM_BANKS):
+                multiply(g, b, w_whole[g], 0)
+
+        for part in range(PARTS):
+            first_bank = part * PART_BANKS
+            for g in range(WHOLE_PASSES, PASSES):
+                for b in range(first_bank, first_bank + PART_BANKS):
+                    multiply(g, b, w_parts[part][g - WHOLE_PASSES], first_bank)
+            for b in range(first_bank, first_bank + PART_BANKS, STORE_BANKS):
                 repeated = results.tile([P, STORE_BANKS, N_BANK, REPEAT], F32)
                 nc.vector.tensor_copy(
                     out=repeated[:, 0], in_=banks[b][:].unsqueeze(2).to_broadcast([P, N_BANK, REPEAT])
@@ -133,7 +146,7 @@ def tile_mora_w_kernel(tc, x, matrix_words, matrix_scales, out):
                 nc.scalar.copy(
                     out=repeated[:, 1], in_=banks[b + 1][:].unsqueeze(2).to_broadcast([P, N_BANK, REPEAT])
                 )
-                first_out = (first_n + b * N_BANK) * REPEAT
+                first_out = b * N_BANK * REPEAT
                 nc.sync.dma_start(
                     out=out_rows[:, first_out : first_out + STORE_BANKS * N_BANK * REPEAT],
                     in_=repeated[:].rearrange("p b n j -> p (b n j)"),

@@ -53,8 +53,8 @@ def tile_mora_w_kernel(tc, x, matrix_words, matrix_scales, out):
         x_all = keep.tile([P, GROUPS, R], BF16)
         nc.sync.dma_start(out=x_all[:], in_=x_groups)
 
-        for a in range(PLANE_SETS):
-            for quadrant in range(QUADRANTS):
+        for quadrant in (2, 3, 0, 1):
+            for a in range(PLANE_SETS):
                 first = 32 * quadrant
                 nc.sync.dma_start(
                     out=w_planes[first : first + PLANES_PER_TILE * SCALE_ROWS, a, :].bitcast(I32),

@@ -55,15 +55,18 @@ def tile_mora_w_kernel(tc, x, matrix_words, matrix_scales, out):
 
         for quadrant in (2, 3, 0, 1):
             for a in range(PLANE_SETS):
-                first = 32 * quadrant
-                nc.sync.dma_start(
-                    out=w_planes[first : first + PLANES_PER_TILE * SCALE_ROWS, a, :].bitcast(I32),
-                    in_=matrix_scales[
-                        a * PLANES_PER_TILE : (a + 1) * PLANES_PER_TILE,
-                        quadrant * SCALE_ROWS : (quadrant + 1) * SCALE_ROWS,
-                        :,
-                    ].bitcast(I32),
-                )
+                pieces = 2 if (quadrant, a) == (1, PLANE_SETS - 1) else 1
+                for piece in range(pieces):
+                    first = 32 * quadrant
+                    columns = slice(piece * (R // pieces), (piece + 1) * (R // pieces))
+                    nc.sync.dma_start(
+                        out=w_planes[first : first + PLANES_PER_TILE * SCALE_ROWS, a, columns].bitcast(I32),
+                        in_=matrix_scales[
+                            a * PLANES_PER_TILE : (a + 1) * PLANES_PER_TILE,
+                            quadrant * SCALE_ROWS : (quadrant + 1) * SCALE_ROWS,
+                            columns,
+                        ].bitcast(I32),
+                    )
 
         def load_words(g, first_bank, banks):
             w_words = keep.tile(

from contextlib import ExitStack

import concourse.mybir as mybir
from concourse.masks import make_identity

BF16 = mybir.dt.bfloat16
F32 = mybir.dt.float32
I32 = mybir.dt.int32
U8 = mybir.dt.uint8
U32 = mybir.dt.uint32
FP8X4 = mybir.dt.float8_e4m3fn_x4

P = 128
PACK = 4
K_PASS = P * PACK
R = 4096
GROUPS = 2
REPEAT = 2
PASSES = R // K_PASS
N_BANK = 512
PSUM_BANKS = 8
SPLIT_PASSES = 2
WHOLE_PASSES = PASSES - SPLIT_PASSES
PARTS = 2
PART_BANKS = PSUM_BANKS // PARTS
STORE_BANKS = 2
X_PIECES = 2
K_PIECE = R // X_PIECES
PASSES_PER_PIECE = K_PIECE // K_PASS
PLANES_PER_TILE = 4
PLANE_SETS = PASSES // PLANES_PER_TILE
QUADRANTS = 4
SCALE_ROWS = 4

FLOPS = 2 * P * R * R


def tile_mora_w_kernel(tc, x, matrix_words, matrix_scales, out):
    nc = tc.nc
    x_groups = x.rearrange("b s (h k) -> (b s) h k", h=GROUPS)
    out_rows = out.rearrange("b s n -> (b s) n")

    with ExitStack() as ctx:
        keep = ctx.enter_context(tc.tile_pool(name="keep", bufs=1))
        results = ctx.enter_context(tc.tile_pool(name="results", bufs=PSUM_BANKS // STORE_BANKS))
        psum = ctx.enter_context(tc.psum_pool(name="psum", bufs=PSUM_BANKS))

        w_planes = keep.tile([P, PLANE_SETS, R], U8, align_bytes=64)
        nc.vector.memset(w_planes[:].rearrange("p a n -> p (a n)").bitcast(I32), 0)
        identity = keep.tile([P, P], BF16)
        make_identity(nc, identity[:])

        x_all = keep.tile([P, GROUPS, R], BF16)
        nc.sync.dma_start(out=x_all[:], in_=x_groups)

        for quadrant in (2, 3, 0, 1):
            for a in range(PLANE_SETS):
                pieces = 2 if (quadrant, a) == (1, PLANE_SETS - 1) else 1
                for piece in range(pieces):
                    first = 32 * quadrant
                    columns = slice(piece * (R // pieces), (piece + 1) * (R // pieces))
                    nc.sync.dma_start(
                        out=w_planes[first : first + PLANES_PER_TILE * SCALE_ROWS, a, columns].bitcast(I32),
                        in_=matrix_scales[
                            a * PLANES_PER_TILE : (a + 1) * PLANES_PER_TILE,
                            quadrant * SCALE_ROWS : (quadrant + 1) * SCALE_ROWS,
                            columns,
                        ].bitcast(I32),
                    )

        def load_words(g, first_bank, banks):
            w_words = keep.tile(
                [P, banks * N_BANK * PACK], U8, name="w_words%d_%d" % (g, first_bank), align_bytes=64
            )
            w_bytes = matrix_words[g].rearrange("p n t -> p (n t)")
            first_byte = first_bank * N_BANK * PACK
            nc.sync.dma_start(
                out=w_words[:].bitcast(I32),
                in_=w_bytes[:, first_byte : first_byte + banks * N_BANK * PACK].bitcast(I32),
            )
            return w_words

        w_whole = [load_words(g, 0, PSUM_BANKS) for g in range(WHOLE_PASSES)]
        w_parts = [
            [load_words(g, part * PART_BANKS, PART_BANKS) for g in range(WHOLE_PASSES, PASSES)]
            for part in range(PARTS)
        ]

        c_codes = keep.tile([P, PASSES, P], U32, align_bytes=64)
        c_scales = keep.tile([P, PASSES, P], U8, align_bytes=64)
        for j in range(X_PIECES):
            c = keep.tile([P, K_PIECE], BF16, name="c%d" % j)
            nc.vector.tensor_tensor(
                out=c[:], in0=x_all[:, 0, j * K_PIECE : (j + 1) * K_PIECE],
                in1=x_all[:, 1, j * K_PIECE : (j + 1) * K_PIECE],
                op=mybir.AluOpType.add,
            )
            grouped = keep.tile([P, PASSES_PER_PIECE, P, PACK], BF16, name="grouped%d" % j, align_bytes=64)
            for i in range(PASSES_PER_PIECE):
                c_t = psum.tile([P, PACK, P], BF16, tag="bank")
                for t in range(PACK):
                    nc.tensor.transpose(
                        c_t[:, t, :], c[:, i * K_PASS + t : (i + 1) * K_PASS : PACK], identity[:]
                    )
                if i % 2 == 0:
                    nc.scalar.copy(out=grouped[:, i], in_=c_t[:].rearrange("p t s -> p s t"))
                else:
                    nc.vector.tensor_copy(out=grouped[:, i], in_=c_t[:].rearrange("p t s -> p s t"))
            passes = slice(j * PASSES_PER_PIECE, (j + 1) * PASSES_PER_PIECE)
            nc.vector.quantize_mx(
                out=c_codes[:, passes, :].rearrange("p g s -> p (g s)").bitcast(FP8X4),
                scales=c_scales[:, passes, :].rearrange("p g s -> p (g s)"),
                in_=grouped[:].rearrange("p g s t -> p (g s t)"),
            )

        banks = []
        for b in range(PSUM_BANKS):
            acc = psum.tile([P, N_BANK], F32, tag="bank", name="acc%d" % b)
            banks.append(acc)

        def multiply(g, b, w_words, first_bank):
            plane_set = g // PLANES_PER_TILE
            plane_start = SCALE_ROWS * (g % PLANES_PER_TILE)
            first_byte = (b - first_bank) * N_BANK * PACK
            nc.tensor.matmul_mx(
                out=banks[b][:],
                lhsT=c_codes[:, g, :].bitcast(FP8X4),
                lhsT_scale=c_scales[:, g, :],
                rhs=w_words[:, first_byte : first_byte + N_BANK * PACK].bitcast(FP8X4),
                rhs_scale=w_planes[plane_start:P, plane_set, b * N_BANK : (b + 1) * N_BANK],
                start=(g == 0),
                stop=(g == PASSES - 1),
            )

        for g in range(WHOLE_PASSES):
            for b in range(PSUM_BANKS):
                multiply(g, b, w_whole[g], 0)

        for part in range(PARTS):
            first_bank = part * PART_BANKS
            for g in range(WHOLE_PASSES, PASSES):
                for b in range(first_bank, first_bank + PART_BANKS):
                    multiply(g, b, w_parts[part][g - WHOLE_PASSES], first_bank)
            for b in range(first_bank, first_bank + PART_BANKS, STORE_BANKS):
                repeated = results.tile([P, STORE_BANKS, N_BANK, REPEAT], F32)
                nc.vector.tensor_copy(
                    out=repeated[:, 0], in_=banks[b][:].unsqueeze(2).to_broadcast([P, N_BANK, REPEAT])
                )
                nc.scalar.copy(
                    out=repeated[:, 1], in_=banks[b + 1][:].unsqueeze(2).to_broadcast([P, N_BANK, REPEAT])
                )
                first_out = b * N_BANK * REPEAT
                nc.sync.dma_start(
                    out=out_rows[:, first_out : first_out + STORE_BANKS * N_BANK * REPEAT],
                    in_=repeated[:].rearrange("p b n j -> p (b n j)"),
                )
